import numpy as np
import ml_dtypes

BF16 = ml_dtypes.bfloat16


def bf(x):
    return np.asarray(x, np.float32).astype(BF16)


def f32(x):
    return np.asarray(x, np.float32)


def f64(x):
    return np.asarray(x).astype(np.float64)


def striped(idx):
    return np.tile(idx.reshape(-1, 16).T, (8, 1))


C, S, T, L, N = 128, 256, 256, 4, 1024


def setup_inputs():
    idx = np.concatenate([np.random.permutation(S) for _ in range(N // S)])
    return {"x": f32(np.random.standard_normal((C, S))), "h": f32(np.random.standard_normal((C, N))), "offs": striped(idx)}


def reference(x, h, offs):
    idx = offs[:16].T.reshape(-1)
    prod = f64(x)[:, idx] * f64(h)
    return prod.reshape(C, T, L).sum(axis=2)

@@ -1,0 +1,42 @@
+import concourse.mybir as mybir
+
+F32 = mybir.dt.float32
+U16 = mybir.dt.uint16
+MULT = mybir.AluOpType.mult
+ADD = mybir.AluOpType.add
+
+LINKS = 128
+SAMPLES = 256
+ENTRIES = 1024
+TAPS = 4
+PIECE = 256
+
+
+def tile_applytimechannel_kernel(tc, x, h, offs, out):
+    nc = tc.nc
+    with tc.tile_pool(name="held", bufs=1) as held:
+        offsets = held.tile([LINKS, ENTRIES // 16], U16, name="offsets")
+        signal = held.tile([LINKS, SAMPLES], F32, name="signal")
+        taps = held.tile([LINKS, ENTRIES], F32, name="taps")
+        weighed = held.tile([LINKS, ENTRIES], F32, name="weighed")
+        received = held.tile([LINKS, ENTRIES // TAPS], F32, name="received")
+
+        nc.sync.dma_start(offsets[:], offs)
+        nc.scalar.dma_start(signal[:], x)
+        nc.sync.dma_start(taps[:], h)
+
+        for first in range(0, ENTRIES, PIECE):
+            nc.vector.tensor_tensor(
+                weighed[:, first : first + PIECE],
+                signal[:].indirect(offsets[:, first // 16 : (first + PIECE) // 16]),
+                taps[:, first : first + PIECE],
+                MULT,
+            )
+
+        nc.vector.tensor_reduce(
+            received[:],
+            weighed[:].rearrange("c (t l) -> c t l", l=TAPS),
+            mybir.AxisListType.X,
+            ADD,
+        )
+        nc.sync.dma_start(out, received[:])

@@ -10,6 +10,7 @@ SAMPLES = 256
 ENTRIES = 1024
 TAPS = 4
 PIECE = 256
+PIECES = ENTRIES // PIECE
 
 
 def tile_applytimechannel_kernel(tc, x, h, offs, out):
@@ -17,19 +18,21 @@ def tile_applytimechannel_kernel(tc, x, h, offs, out):
     with tc.tile_pool(name="held", bufs=1) as held:
         offsets = held.tile([LINKS, ENTRIES // 16], U16, name="offsets")
         signal = held.tile([LINKS, SAMPLES], F32, name="signal")
-        taps = held.tile([LINKS, ENTRIES], F32, name="taps")
+        taps = [held.tile([LINKS, PIECE], F32, name=f"taps{k}") for k in range(PIECES)]
         weighed = held.tile([LINKS, ENTRIES], F32, name="weighed")
         received = held.tile([LINKS, ENTRIES // TAPS], F32, name="received")
 
         nc.sync.dma_start(offsets[:], offs)
         nc.scalar.dma_start(signal[:], x)
-        nc.sync.dma_start(taps[:], h)
+        for k in range(PIECES):
+            queue = nc.sync if k % 2 == 0 else nc.scalar
+            queue.dma_start(taps[k][:], h[:, k * PIECE : (k + 1) * PIECE])
 
-        for first in range(0, ENTRIES, PIECE):
+        for k in range(PIECES):
             nc.vector.tensor_tensor(
-                weighed[:, first : first + PIECE],
-                signal[:].indirect(offsets[:, first // 16 : (first + PIECE) // 16]),
-                taps[:, first : first + PIECE],
+                weighed[:, k * PIECE : (k + 1) * PIECE],
+                signal[:].indirect(offsets[:, k * PIECE // 16 : (k + 1) * PIECE // 16]),
+                taps[k][:],
                 MULT,
             )
 

@@ -20,6 +20,7 @@ def tile_applytimechannel_kernel(tc, x, h, offs, out):
         signal = held.tile([LINKS, SAMPLES], F32, name="signal")
         taps = [held.tile([LINKS, PIECE], F32, name=f"taps{k}") for k in range(PIECES)]
         weighed = held.tile([LINKS, ENTRIES], F32, name="weighed")
+        halves = held.tile([LINKS, ENTRIES // 2], F32, name="halves")
         received = held.tile([LINKS, ENTRIES // TAPS], F32, name="received")
 
         nc.sync.dma_start(offsets[:], offs)
@@ -36,10 +37,8 @@ def tile_applytimechannel_kernel(tc, x, h, offs, out):
                 MULT,
             )
 
-        nc.vector.tensor_reduce(
-            received[:],
-            weighed[:].rearrange("c (t l) -> c t l", l=TAPS),
-            mybir.AxisListType.X,
-            ADD,
-        )
+        by_tap = weighed[:].rearrange("c (t l) -> c t l", l=TAPS)
+        by_half = halves[:].rearrange("c (t i) -> c t i", i=2)
+        nc.vector.tensor_tensor(by_half, by_tap[:, :, 0:2], by_tap[:, :, 2:4], ADD)
+        nc.vector.tensor_tensor(received[:], by_half[:, :, 0], by_half[:, :, 1], ADD)
         nc.sync.dma_start(out, received[:])

@@ -11,6 +11,8 @@ ENTRIES = 1024
 TAPS = 4
 PIECE = 256
 PIECES = ENTRIES // PIECE
+OUTPUTS = ENTRIES // TAPS
+SUMS = PIECE // TAPS
 
 
 def tile_applytimechannel_kernel(tc, x, h, offs, out):
@@ -20,8 +22,7 @@ def tile_applytimechannel_kernel(tc, x, h, offs, out):
         signal = held.tile([LINKS, SAMPLES], F32, name="signal")
         taps = [held.tile([LINKS, PIECE], F32, name=f"taps{k}") for k in range(PIECES)]
         weighed = held.tile([LINKS, ENTRIES], F32, name="weighed")
-        halves = held.tile([LINKS, ENTRIES // 2], F32, name="halves")
-        received = held.tile([LINKS, ENTRIES // TAPS], F32, name="received")
+        received = held.tile([LINKS, OUTPUTS], F32, name="received")
 
         nc.sync.dma_start(offsets[:], offs)
         nc.scalar.dma_start(signal[:], x)
@@ -29,7 +30,9 @@ def tile_applytimechannel_kernel(tc, x, h, offs, out):
             queue = nc.sync if k % 2 == 0 else nc.scalar
             queue.dma_start(taps[k][:], h[:, k * PIECE : (k + 1) * PIECE])
 
-        for k in range(PIECES):
+        by_sample = weighed[:].rearrange("c (t l) -> c t l", l=TAPS)
+
+        def weigh(k):
             nc.vector.tensor_tensor(
                 weighed[:, k * PIECE : (k + 1) * PIECE],
                 signal[:].indirect(offsets[:, k * PIECE // 16 : (k + 1) * PIECE // 16]),
@@ -37,8 +40,16 @@ def tile_applytimechannel_kernel(tc, x, h, offs, out):
                 MULT,
             )
 
-        by_tap = weighed[:].rearrange("c (t l) -> c t l", l=TAPS)
-        by_half = halves[:].rearrange("c (t i) -> c t i", i=2)
-        nc.vector.tensor_tensor(by_half, by_tap[:, :, 0:2], by_tap[:, :, 2:4], ADD)
-        nc.vector.tensor_tensor(received[:], by_half[:, :, 0], by_half[:, :, 1], ADD)
-        nc.sync.dma_start(out, received[:])
+        def sum_and_store(k):
+            columns = slice(k * SUMS, (k + 1) * SUMS)
+            nc.vector.tensor_reduce(
+                received[:, columns], by_sample[:, columns, :], mybir.AxisListType.X, ADD
+            )
+            queue = nc.sync if k % 2 == 1 else nc.scalar
+            queue.dma_start(out[:, columns], received[:, columns])
+
+        weigh(0)
+        for k in range(1, PIECES):
+            weigh(k)
+            sum_and_store(k - 1)
+        sum_and_store(PIECES - 1)

@@ -12,7 +12,7 @@ TAPS = 4
 PIECE = 256
 PIECES = ENTRIES // PIECE
 OUTPUTS = ENTRIES // TAPS
-SUMS = PIECE // TAPS
+LAST = OUTPUTS - PIECE // TAPS
 
 
 def tile_applytimechannel_kernel(tc, x, h, offs, out):
@@ -30,9 +30,7 @@ def tile_applytimechannel_kernel(tc, x, h, offs, out):
             queue = nc.sync if k % 2 == 0 else nc.scalar
             queue.dma_start(taps[k][:], h[:, k * PIECE : (k + 1) * PIECE])
 
-        by_sample = weighed[:].rearrange("c (t l) -> c t l", l=TAPS)
-
-        def weigh(k):
+        for k in range(PIECES):
             nc.vector.tensor_tensor(
                 weighed[:, k * PIECE : (k + 1) * PIECE],
                 signal[:].indirect(offsets[:, k * PIECE // 16 : (k + 1) * PIECE // 16]),
@@ -40,16 +38,9 @@ def tile_applytimechannel_kernel(tc, x, h, offs, out):
                 MULT,
             )
 
-        def sum_and_store(k):
-            columns = slice(k * SUMS, (k + 1) * SUMS)
+        by_sample = weighed[:].rearrange("c (t l) -> c t l", l=TAPS)
+        for first, end, queue in ((0, LAST, nc.scalar), (LAST, OUTPUTS, nc.sync)):
             nc.vector.tensor_reduce(
-                received[:, columns], by_sample[:, columns, :], mybir.AxisListType.X, ADD
+                received[:, first:end], by_sample[:, first:end, :], mybir.AxisListType.X, ADD
             )
-            queue = nc.sync if k % 2 == 1 else nc.scalar
-            queue.dma_start(out[:, columns], received[:, columns])
-
-        weigh(0)
-        for k in range(1, PIECES):
-            weigh(k)
-            sum_and_store(k - 1)
-        sum_and_store(PIECES - 1)
+            queue.dma_start(out[:, first:end], received[:, first:end])

@@ -10,9 +10,10 @@ SAMPLES = 256
 ENTRIES = 1024
 TAPS = 4
 PIECE = 256
-PIECES = ENTRIES // PIECE
 OUTPUTS = ENTRIES // TAPS
 LAST = OUTPUTS - PIECE // TAPS
+BOUNDS = [0, PIECE // 4] + list(range(PIECE, ENTRIES + 1, PIECE))
+PIECES = list(zip(BOUNDS[:-1], BOUNDS[1:]))
 
 
 def tile_applytimechannel_kernel(tc, x, h, offs, out):
@@ -20,20 +21,20 @@ def tile_applytimechannel_kernel(tc, x, h, offs, out):
     with tc.tile_pool(name="held", bufs=1) as held:
         offsets = held.tile([LINKS, ENTRIES // 16], U16, name="offsets")
         signal = held.tile([LINKS, SAMPLES], F32, name="signal")
-        taps = [held.tile([LINKS, PIECE], F32, name=f"taps{k}") for k in range(PIECES)]
+        taps = [held.tile([LINKS, end - first], F32, name=f"taps{first}") for first, end in PIECES]
         weighed = held.tile([LINKS, ENTRIES], F32, name="weighed")
         received = held.tile([LINKS, OUTPUTS], F32, name="received")
 
         nc.sync.dma_start(offsets[:], offs)
         nc.scalar.dma_start(signal[:], x)
-        for k in range(PIECES):
+        for k, (first, end) in enumerate(PIECES):
             queue = nc.sync if k % 2 == 0 else nc.scalar
-            queue.dma_start(taps[k][:], h[:, k * PIECE : (k + 1) * PIECE])
+            queue.dma_start(taps[k][:], h[:, first:end])
 
-        for k in range(PIECES):
+        for k, (first, end) in enumerate(PIECES):
             nc.vector.tensor_tensor(
-                weighed[:, k * PIECE : (k + 1) * PIECE],
-                signal[:].indirect(offsets[:, k * PIECE // 16 : (k + 1) * PIECE // 16]),
+                weighed[:, first:end],
+                signal[:].indirect(offsets[:, first // 16 : end // 16]),
                 taps[k][:],
                 MULT,
             )

@@ -14,6 +14,7 @@ OUTPUTS = ENTRIES // TAPS
 LAST = OUTPUTS - PIECE // TAPS
 BOUNDS = [0, PIECE // 4] + list(range(PIECE, ENTRIES + 1, PIECE))
 PIECES = list(zip(BOUNDS[:-1], BOUNDS[1:]))
+LOADS = PIECES[:-2] + [(PIECES[-2][0], PIECES[-1][1])]
 
 
 def tile_applytimechannel_kernel(tc, x, h, offs, out):
@@ -21,21 +22,21 @@ def tile_applytimechannel_kernel(tc, x, h, offs, out):
     with tc.tile_pool(name="held", bufs=1) as held:
         offsets = held.tile([LINKS, ENTRIES // 16], U16, name="offsets")
         signal = held.tile([LINKS, SAMPLES], F32, name="signal")
-        taps = [held.tile([LINKS, end - first], F32, name=f"taps{first}") for first, end in PIECES]
+        taps = held.tile([LINKS, ENTRIES], F32, name="taps")
         weighed = held.tile([LINKS, ENTRIES], F32, name="weighed")
         received = held.tile([LINKS, OUTPUTS], F32, name="received")
 
         nc.sync.dma_start(offsets[:], offs)
         nc.scalar.dma_start(signal[:], x)
-        for k, (first, end) in enumerate(PIECES):
+        for k, (first, end) in enumerate(LOADS):
             queue = nc.sync if k % 2 == 0 else nc.scalar
-            queue.dma_start(taps[k][:], h[:, first:end])
+            queue.dma_start(taps[:, first:end], h[:, first:end])
 
-        for k, (first, end) in enumerate(PIECES):
+        for first, end in PIECES:
             nc.vector.tensor_tensor(
                 weighed[:, first:end],
                 signal[:].indirect(offsets[:, first // 16 : end // 16]),
-                taps[k][:],
+                taps[:, first:end],
                 MULT,
             )
 

import concourse.mybir as mybir

F32 = mybir.dt.float32
U16 = mybir.dt.uint16
MULT = mybir.AluOpType.mult
ADD = mybir.AluOpType.add

LINKS = 128
SAMPLES = 256
ENTRIES = 1024
TAPS = 4
PIECE = 256
OUTPUTS = ENTRIES // TAPS
LAST = OUTPUTS - PIECE // TAPS
BOUNDS = [0, PIECE // 4] + list(range(PIECE, ENTRIES + 1, PIECE))
PIECES = list(zip(BOUNDS[:-1], BOUNDS[1:]))
LOADS = PIECES[:-2] + [(PIECES[-2][0], PIECES[-1][1])]


def tile_applytimechannel_kernel(tc, x, h, offs, out):
    nc = tc.nc
    with tc.tile_pool(name="held", bufs=1) as held:
        offsets = held.tile([LINKS, ENTRIES // 16], U16, name="offsets")
        signal = held.tile([LINKS, SAMPLES], F32, name="signal")
        taps = held.tile([LINKS, ENTRIES], F32, name="taps")
        weighed = held.tile([LINKS, ENTRIES], F32, name="weighed")
        received = held.tile([LINKS, OUTPUTS], F32, name="received")

        nc.sync.dma_start(offsets[:], offs)
        nc.scalar.dma_start(signal[:], x)
        for k, (first, end) in enumerate(LOADS):
            queue = nc.sync if k % 2 == 0 else nc.scalar
            queue.dma_start(taps[:, first:end], h[:, first:end])

        for first, end in PIECES:
            nc.vector.tensor_tensor(
                weighed[:, first:end],
                signal[:].indirect(offsets[:, first // 16 : end // 16]),
                taps[:, first:end],
                MULT,
            )

        by_sample = weighed[:].rearrange("c (t l) -> c t l", l=TAPS)
        for first, end, queue in ((0, LAST, nc.scalar), (LAST, OUTPUTS, nc.sync)):
            nc.vector.tensor_reduce(
                received[:, first:end], by_sample[:, first:end, :], mybir.AxisListType.X, ADD
            )
            queue.dma_start(out[:, first:end], received[:, first:end])
